import numpy as np
import ml_dtypes


def mxq(x, axis, fmt="e4m3"):
    dtype, down = {"e4m3": (ml_dtypes.float8_e4m3fn, 7), "e5m2": (ml_dtypes.float8_e5m2, 14)}[fmt]
    v = np.moveaxis(np.asarray(x, np.float32).astype(ml_dtypes.bfloat16).astype(np.float64), axis, -1)
    blocks = v.reshape(v.shape[:-1] + (-1, 32))
    amax = np.abs(blocks).max(-1, keepdims=True)
    byte = np.maximum(np.where(amax > 0, np.frexp(amax)[1] - 1 + 127, 0) - down, 1)
    scale = np.exp2(byte - 127.0)
    codes = (blocks / scale).astype(np.float32).astype(dtype).astype(np.float64)
    return np.moveaxis((codes * scale).reshape(v.shape), -1, axis)


WIDE = False


def mx_kscale(k):
    if not WIDE:
        return np.ones(k)
    levels = np.array([10, -10, 5, -5, 0])
    a = np.random.permutation(np.resize(levels, k // 512 * 4)).reshape(k // 512, 4)
    idx = np.arange(k)
    return np.exp2(a[idx // 512, idx % 128 // 32])


BF16 = ml_dtypes.bfloat16


def bf(x):
    return np.asarray(x, np.float32).astype(BF16)


def f64(x):
    return np.asarray(x).astype(np.float64)


N, D, T, O = 1024, 512, 1024, 512
LEAKY_SLOPE = 0.01
P_EDGE = 0.25
ZS = np.sqrt(N) / 8.0


def setup_inputs():
    s = mx_kscale(D)
    edges = np.random.random((N, N)) < P_EDGE
    return {"A1": bf((0.1 + 0.9 * np.random.random((N, N))) * edges + np.eye(N)),
            "Hn": bf(np.random.standard_normal((N, D)) * s),
            "Wout": bf(np.random.standard_normal((D, O)) * ZS / np.sqrt(D) / s[:, None]),
            "bout": bf(0.1 * np.random.standard_normal(O) - 0.2)}


def reference(A1, Hn, Wout, bout):
    A = f64(A1)
    d = np.power(A.sum(axis=1), -0.5)
    A_hat = A * d[:, None] * d[None, :]
    Z = (mxq(f64(Hn), 1, "e4m3") @ mxq(f64(Wout), 0, "e4m3")) + f64(bout)
    y = mxq(A_hat, 1, "e4m3") @ mxq(Z, 0, "e4m3")
    return np.where(y >= 0, y, LEAKY_SLOPE * y)

@@ -1,0 +1,207 @@
+from contextlib import ExitStack
+
+import concourse.mybir as mybir
+from concourse.masks import make_identity
+
+F32 = mybir.dt.float32
+BF16 = mybir.dt.bfloat16
+U32 = mybir.dt.uint32
+U8 = mybir.dt.uint8
+FP8X4 = mybir.dt.float8_e4m3fn_x4
+ACT = mybir.ActivationFunctionType
+ALU = mybir.AluOpType
+
+P = 128
+PACK = 4
+K_PASS = P * PACK
+NODES = 1024
+FEATS = 512
+OUTS = 512
+NODE_TILES = NODES // P
+NODE_PASSES = NODES // K_PASS
+OUT_CHUNKS = OUTS // P
+BANK_F32 = 512
+LEAKY_SLOPE = 0.01
+ROWSUMS_ON_SCALAR = 6
+
+FLOPS = 2 * NODES * FEATS * OUTS + 2 * NODES * NODES * OUTS
+
+
+def tile_gcnlayer_pb_kernel(tc, A1, Hn, Wout, bout, out):
+    nc = tc.nc
+    with ExitStack() as ctx:
+        keep = ctx.enter_context(tc.tile_pool(name="keep", bufs=1))
+        work = ctx.enter_context(tc.tile_pool(name="work", bufs=3))
+        psum = ctx.enter_context(tc.psum_pool(name="psum", bufs=3))
+        psum_keep = ctx.enter_context(tc.psum_pool(name="psum_keep", bufs=1))
+
+        one = keep.tile([P, 1], F32)
+        nc.vector.memset(one[:], 1.0)
+        warm = keep.tile([P, 1], F32)
+        nc.scalar.activation(out=warm[:], in_=one[:], func=ACT.Sqrt)
+        ident_f32 = keep.tile([P, P], F32)
+        make_identity(nc, ident_f32[:])
+        ident_bf16 = keep.tile([P, P], BF16)
+        make_identity(nc, ident_bf16[:])
+
+        w_raw = keep.tile([P, PACK, OUTS], BF16)
+        nc.sync.dma_start(
+            out=w_raw[:].rearrange("q (u e) c -> q u e c", u=2),
+            in_=Wout.rearrange("(u q e) c -> q u e c", u=2, e=2),
+        )
+        hn_raw = keep.tile([P, NODE_TILES, FEATS], BF16)
+        hn_view = Hn.rearrange("(n p) k -> p n k", p=P)
+        for half in range(2):
+            tiles = slice(4 * half, 4 * half + 4)
+            nc.sync.dma_start(out=hn_raw[:, tiles, :], in_=hn_view[:, tiles, :])
+        bias = keep.tile([P, OUTS], BF16)
+        nc.gpsimd.dma_start(out=bias[:], in_=bout.partition_broadcast(P))
+        a_raw = []
+        for m in range(NODE_TILES):
+            a_tile = keep.tile([P, NODES], BF16, name="a_raw%d" % m)
+            nc.sync.dma_start(out=a_tile[:], in_=A1[m * P : (m + 1) * P, :])
+            a_raw.append(a_tile)
+
+        w_grouped = keep.tile([P, OUTS, PACK], BF16, align_bytes=64)
+        nc.vector.tensor_copy(
+            out=w_grouped[:].rearrange("p (c i) t -> p c t i", i=4),
+            in_=w_raw[:].rearrange("p t (c i) -> p c t i", i=4),
+        )
+        w_codes = keep.tile([P, OUTS], U32, align_bytes=64)
+        w_scales = keep.tile([P, OUTS], U8, align_bytes=64)
+        nc.vector.quantize_mx(
+            out=w_codes[:].bitcast(FP8X4),
+            scales=w_scales[:],
+            in_=w_grouped[:].rearrange("p c t -> p (c t)"),
+        )
+
+        hn_words = hn_raw[:].bitcast(F32)
+        hn_grouped = keep.tile([P, NODE_TILES, P, PACK], BF16, align_bytes=64)
+        hn_grouped_words = hn_grouped[:].bitcast(F32)
+        hn_codes = keep.tile([P, NODES], U32, align_bytes=64)
+        hn_scales = keep.tile([P, NODES], U8, align_bytes=64)
+        for half in range(2):
+            for pair in range(2 * half, 2 * half + 2):
+                hn_t = psum.tile([P, 2, 2, P], F32, tag="transposed")
+                for n2 in range(2):
+                    for u in range(2):
+                        nc.tensor.transpose(
+                            out=hn_t[:, n2, u, :],
+                            in_=hn_words[:, 2 * pair + n2, u * P : (u + 1) * P],
+                            identity=ident_f32[:],
+                        )
+                nc.scalar.copy(
+                    out=hn_grouped_words[:, 2 * pair : 2 * pair + 2, :, :],
+                    in_=hn_t[:].rearrange("p n u r -> p n r u"),
+                )
+            cols = slice(half * K_PASS, (half + 1) * K_PASS)
+            nc.vector.quantize_mx(
+                out=hn_codes[:, cols].bitcast(FP8X4),
+                scales=hn_scales[:, cols],
+                in_=hn_grouped[:, 4 * half : 4 * half + 4, :, :].rearrange("p n r t -> p (n r t)"),
+            )
+
+        sums_scalar = keep.tile([P, ROWSUMS_ON_SCALAR], F32)
+        sums_vector = keep.tile([P, NODE_TILES - ROWSUMS_ON_SCALAR], F32)
+        for m in range(NODE_TILES):
+            if m < ROWSUMS_ON_SCALAR:
+                unread = work.tile([P, NODES], BF16)
+                nc.scalar.activation(
+                    out=unread[:], in_=a_raw[m][:], func=ACT.Copy, accum_out=sums_scalar[:, m : m + 1]
+                )
+            else:
+                k = m - ROWSUMS_ON_SCALAR
+                nc.vector.tensor_reduce(
+                    out=sums_vector[:, k : k + 1], in_=a_raw[m][:], axis=mybir.AxisListType.X, op=ALU.add
+                )
+
+        z_grouped = keep.tile([P, NODE_PASSES, OUTS, PACK], BF16, align_bytes=64)
+        z_codes = keep.tile([P, NODE_PASSES, OUTS], U32, align_bytes=64)
+        z_scales = keep.tile([P, NODE_PASSES, OUTS], U8, align_bytes=64)
+        for g in range(NODE_PASSES):
+            for c in range(OUT_CHUNKS):
+                o_cols = slice(c * P, (c + 1) * P)
+                z_bank = psum.tile([P, PACK, P], F32, tag="product")
+                for t in range(PACK):
+                    n_cols = slice((PACK * g + t) * P, (PACK * g + t + 1) * P)
+                    nc.tensor.matmul_mx(
+                        out=z_bank[:, t, :],
+                        lhsT=hn_codes[:, n_cols].bitcast(FP8X4),
+                        lhsT_scale=hn_scales[:, n_cols],
+                        rhs=w_codes[:, o_cols].bitcast(FP8X4),
+                        rhs_scale=w_scales[:, o_cols],
+                        start=True,
+                        stop=True,
+                    )
+                nc.vector.tensor_tensor(
+                    out=z_grouped[:, g, o_cols, :],
+                    in0=z_bank[:].rearrange("p t o -> p o t"),
+                    in1=bias[:, o_cols].unsqueeze(2).to_broadcast([P, P, PACK]),
+                    op=ALU.add,
+                )
+            nc.vector.quantize_mx(
+                out=z_codes[:, g, :].bitcast(FP8X4),
+                scales=z_scales[:, g, :],
+                in_=z_grouped[:, g, :, :].rearrange("p o t -> p (o t)"),
+            )
+
+        root = keep.tile([P, NODE_TILES], F32)
+        nc.scalar.activation(out=root[:, :ROWSUMS_ON_SCALAR], in_=sums_scalar[:], func=ACT.Sqrt)
+        nc.scalar.activation(out=root[:, ROWSUMS_ON_SCALAR:], in_=sums_vector[:], func=ACT.Sqrt)
+        d = keep.tile([P, NODE_TILES], F32)
+        nc.vector.reciprocal(out=d[:], in_=root[:])
+        d_repeated = keep.tile([P, NODE_TILES, P], F32)
+        nc.vector.tensor_copy(out=d_repeated[:], in_=d[:].unsqueeze(2).to_broadcast([P, NODE_TILES, P]))
+        d_row = []
+        for h in range(NODES // BANK_F32):
+            d_bank = psum_keep.tile([P, BANK_F32], F32, name="d_row%d" % h)
+            for q in range(BANK_F32 // P):
+                nc.tensor.transpose(
+                    out=d_bank[:, q * P : (q + 1) * P],
+                    in_=d_repeated[:, h * (BANK_F32 // P) + q, :],
+                    identity=ident_f32[:],
+                )
+            d_row.append(d_bank)
+
+        for m in range(NODE_TILES):
+            a_hat = work.tile([P, NODES], BF16)
+            for h in range(NODES // BANK_F32):
+                j_cols = slice(h * BANK_F32, (h + 1) * BANK_F32)
+                nc.vector.scalar_tensor_tensor(
+                    out=a_hat[:, j_cols],
+                    in0=a_raw[m][:, j_cols],
+                    scalar=d[:, m : m + 1],
+                    in1=d_row[h][:],
+                    op0=ALU.mult,
+                    op1=ALU.mult,
+                )
+            a_t = psum.tile([P, NODE_PASSES, PACK, P], BF16, tag="transposed")
+            for g in range(NODE_PASSES):
+                for t in range(PACK):
+                    j0 = (PACK * g + t) * P
+                    nc.tensor.transpose(out=a_t[:, g, t, :], in_=a_hat[:, j0 : j0 + P], identity=ident_bf16[:])
+            a_grouped = work.tile([P, NODE_PASSES, P, PACK], BF16, align_bytes=64)
+            nc.scalar.copy(out=a_grouped[:], in_=a_t[:].rearrange("p g t i -> p g i t"))
+            a_codes = work.tile([P, NODE_PASSES, P], U32, align_bytes=64)
+            a_scales = work.tile([P, NODE_PASSES, P], U8, align_bytes=64)
+            nc.vector.quantize_mx(
+                out=a_codes[:].rearrange("p g i -> p (g i)").bitcast(FP8X4),
+                scales=a_scales[:].rearrange("p g i -> p (g i)"),
+                in_=a_grouped[:].rearrange("p g i t -> p (g i t)"),
+            )
+            y = psum.tile([P, OUTS], F32, tag="product")
+            for g in range(NODE_PASSES):
+                nc.tensor.matmul_mx(
+                    out=y[:],
+                    lhsT=a_codes[:, g, :].bitcast(FP8X4),
+                    lhsT_scale=a_scales[:, g, :],
+                    rhs=z_codes[:, g, :].bitcast(FP8X4),
+                    rhs_scale=z_scales[:, g, :],
+                    start=(g == 0),
+                    stop=(g == NODE_PASSES - 1),
+                )
+            y_small = work.tile([P, OUTS], F32)
+            nc.scalar.mul(out=y_small[:], in_=y[:], mul=LEAKY_SLOPE)
+            result = work.tile([P, OUTS], F32)
+            nc.vector.tensor_tensor(out=result[:], in0=y[:], in1=y_small[:], op=ALU.max)
+            nc.sync.dma_start(out=out[m * P : (m + 1) * P, :], in_=result[:])

@@ -18,11 +18,13 @@ NODES = 1024
 FEATS = 512
 OUTS = 512
 NODE_TILES = NODES // P
-NODE_PASSES = NODES // K_PASS
+HALVES = NODES // K_PASS
+TILES_PER_HALF = NODE_TILES // HALVES
 OUT_CHUNKS = OUTS // P
-BANK_F32 = 512
 LEAKY_SLOPE = 0.01
-ROWSUMS_ON_SCALAR = 6
+Z_BANKS_AHEAD = 2
+QUANTISE_LAG = 2
+RELU_LAG = 2
 
 FLOPS = 2 * NODES * FEATS * OUTS + 2 * NODES * NODES * OUTS
 
@@ -34,33 +36,42 @@ def tile_gcnlayer_pb_kernel(tc, A1, Hn, Wout, bout, out):
         work = ctx.enter_context(tc.tile_pool(name="work", bufs=3))
         psum = ctx.enter_context(tc.psum_pool(name="psum", bufs=3))
         psum_keep = ctx.enter_context(tc.psum_pool(name="psum_keep", bufs=1))
+        ctx.enter_context(tc.manual_schedule())
 
         one = keep.tile([P, 1], F32)
         nc.vector.memset(one[:], 1.0)
         warm = keep.tile([P, 1], F32)
         nc.scalar.activation(out=warm[:], in_=one[:], func=ACT.Sqrt)
+        bias_padded = keep.tile([P, OUTS], BF16)
+        nc.vector.memset(bias_padded[:], 0.0)
+        ones_bf16 = keep.tile([P, P], BF16)
+        nc.vector.memset(ones_bf16[:], 1.0)
         ident_f32 = keep.tile([P, P], F32)
-        make_identity(nc, ident_f32[:])
+        nc.vector.memset(ident_f32[:], 0.0)
+        make_identity(nc, ident_f32[:], nomemset=True)
         ident_bf16 = keep.tile([P, P], BF16)
-        make_identity(nc, ident_bf16[:])
+        nc.vector.memset(ident_bf16[:], 0.0)
+        make_identity(nc, ident_bf16[:], nomemset=True)
 
+        a_raw = [keep.tile([P, NODES], BF16, name="a_raw%d" % m) for m in range(NODE_TILES)]
         w_raw = keep.tile([P, PACK, OUTS], BF16)
+        hn_raw = keep.tile([P, NODE_TILES, FEATS], BF16)
+        hn_view = Hn.rearrange("(n p) k -> p n k", p=P)
+        nc.sync.dma_start(out=bias_padded[0:1, :], in_=bout.unsqueeze(0))
         nc.sync.dma_start(
             out=w_raw[:].rearrange("q (u e) c -> q u e c", u=2),
             in_=Wout.rearrange("(u q e) c -> q u e c", u=2, e=2),
         )
-        hn_raw = keep.tile([P, NODE_TILES, FEATS], BF16)
-        hn_view = Hn.rearrange("(n p) k -> p n k", p=P)
-        for half in range(2):
-            tiles = slice(4 * half, 4 * half + 4)
+        for half in range(HALVES):
+            tiles = slice(TILES_PER_HALF * half, TILES_PER_HALF * (half + 1))
             nc.sync.dma_start(out=hn_raw[:, tiles, :], in_=hn_view[:, tiles, :])
-        bias = keep.tile([P, OUTS], BF16)
-        nc.gpsimd.dma_start(out=bias[:], in_=bout.partition_broadcast(P))
-        a_raw = []
         for m in range(NODE_TILES):
-            a_tile = keep.tile([P, NODES], BF16, name="a_raw%d" % m)
-            nc.sync.dma_start(out=a_tile[:], in_=A1[m * P : (m + 1) * P, :])
-            a_raw.append(a_tile)
+            nc.sync.dma_start(out=a_raw[m][:], in_=A1[m * P : (m + 1) * P, :])
+
+        bias_bank = psum.tile([P, OUTS], F32, tag="product")
+        nc.tensor.matmul(out=bias_bank[:], lhsT=ones_bf16[:], rhs=bias_padded[:], start=True, stop=True)
+        bias = keep.tile([P, OUTS], F32)
+        nc.scalar.copy(out=bias[:], in_=bias_bank[:])
 
         w_grouped = keep.tile([P, OUTS, PACK], BF16, align_bytes=64)
         nc.vector.tensor_copy(
@@ -80,7 +91,7 @@ def tile_gcnlayer_pb_kernel(tc, A1, Hn, Wout, bout, out):
         hn_grouped_words = hn_grouped[:].bitcast(F32)
         hn_codes = keep.tile([P, NODES], U32, align_bytes=64)
         hn_scales = keep.tile([P, NODES], U8, align_bytes=64)
-        for half in range(2):
+        for half in range(HALVES):
             for pair in range(2 * half, 2 * half + 2):
                 hn_t = psum.tile([P, 2, 2, P], F32, tag="transposed")
                 for n2 in range(2):
@@ -98,110 +109,162 @@ def tile_gcnlayer_pb_kernel(tc, A1, Hn, Wout, bout, out):
             nc.vector.quantize_mx(
                 out=hn_codes[:, cols].bitcast(FP8X4),
                 scales=hn_scales[:, cols],
-                in_=hn_grouped[:, 4 * half : 4 * half + 4, :, :].rearrange("p n r t -> p (n r t)"),
+                in_=hn_grouped[:, TILES_PER_HALF * half : TILES_PER_HALF * (half + 1), :, :].rearrange(
+                    "p n r t -> p (n r t)"
+                ),
             )
 
-        sums_scalar = keep.tile([P, ROWSUMS_ON_SCALAR], F32)
-        sums_vector = keep.tile([P, NODE_TILES - ROWSUMS_ON_SCALAR], F32)
-        for m in range(NODE_TILES):
-            if m < ROWSUMS_ON_SCALAR:
-                unread = work.tile([P, NODES], BF16)
-                nc.scalar.activation(
-                    out=unread[:], in_=a_raw[m][:], func=ACT.Copy, accum_out=sums_scalar[:, m : m + 1]
-                )
-            else:
-                k = m - ROWSUMS_ON_SCALAR
-                nc.vector.tensor_reduce(
-                    out=sums_vector[:, k : k + 1], in_=a_raw[m][:], axis=mybir.AxisListType.X, op=ALU.add
-                )
+        root = keep.tile([P, NODE_TILES], F32)
+        sums_scalar = keep.tile([P, TILES_PER_HALF], F32)
+        for m in range(TILES_PER_HALF):
+            unread = work.tile([P, NODES], BF16)
+            nc.scalar.activation(out=unread[:], in_=a_raw[m][:], func=ACT.Copy, accum_out=sums_scalar[:, m : m + 1])
+        nc.scalar.activation(out=root[:, :TILES_PER_HALF], in_=sums_scalar[:], func=ACT.Sqrt)
 
-        z_grouped = keep.tile([P, NODE_PASSES, OUTS, PACK], BF16, align_bytes=64)
-        z_codes = keep.tile([P, NODE_PASSES, OUTS], U32, align_bytes=64)
-        z_scales = keep.tile([P, NODE_PASSES, OUTS], U8, align_bytes=64)
-        for g in range(NODE_PASSES):
-            for c in range(OUT_CHUNKS):
-                o_cols = slice(c * P, (c + 1) * P)
-                z_bank = psum.tile([P, PACK, P], F32, tag="product")
-                for t in range(PACK):
-                    n_cols = slice((PACK * g + t) * P, (PACK * g + t + 1) * P)
-                    nc.tensor.matmul_mx(
-                        out=z_bank[:, t, :],
-                        lhsT=hn_codes[:, n_cols].bitcast(FP8X4),
-                        lhsT_scale=hn_scales[:, n_cols],
-                        rhs=w_codes[:, o_cols].bitcast(FP8X4),
-                        rhs_scale=w_scales[:, o_cols],
-                        start=True,
-                        stop=True,
-                    )
-                nc.vector.tensor_tensor(
-                    out=z_grouped[:, g, o_cols, :],
-                    in0=z_bank[:].rearrange("p t o -> p o t"),
-                    in1=bias[:, o_cols].unsqueeze(2).to_broadcast([P, P, PACK]),
-                    op=ALU.add,
+        z_grouped = keep.tile([P, HALVES, OUTS, PACK], BF16, align_bytes=64)
+        z_codes = keep.tile([P, HALVES, OUTS], U32, align_bytes=64)
+        z_scales = keep.tile([P, HALVES, OUTS], U8, align_bytes=64)
+        z_banks = []
+
+        def first_product(bank):
+            g, c = divmod(bank, OUT_CHUNKS)
+            z_bank = psum.tile([P, PACK, P], F32, tag="product")
+            for t in range(PACK):
+                n_cols = slice((PACK * g + t) * P, (PACK * g + t + 1) * P)
+                nc.tensor.matmul_mx(
+                    out=z_bank[:, t, :],
+                    lhsT=hn_codes[:, n_cols].bitcast(FP8X4),
+                    lhsT_scale=hn_scales[:, n_cols],
+                    rhs=w_codes[:, c * P : (c + 1) * P].bitcast(FP8X4),
+                    rhs_scale=w_scales[:, c * P : (c + 1) * P],
+                    start=True,
+                    stop=True,
                 )
+            z_banks.append(z_bank)
+
+        def add_bias(bank):
+            g, c = divmod(bank, OUT_CHUNKS)
+            o_cols = slice(c * P, (c + 1) * P)
+            nc.vector.tensor_tensor(
+                out=z_grouped[:, g, o_cols, :],
+                in0=z_banks[bank][:].rearrange("p t o -> p o t"),
+                in1=bias[:, o_cols].unsqueeze(2).to_broadcast([P, P, PACK]),
+                op=ALU.add,
+            )
+
+        def quantise_z(g):
             nc.vector.quantize_mx(
                 out=z_codes[:, g, :].bitcast(FP8X4),
                 scales=z_scales[:, g, :],
                 in_=z_grouped[:, g, :, :].rearrange("p o t -> p (o t)"),
             )
 
-        root = keep.tile([P, NODE_TILES], F32)
-        nc.scalar.activation(out=root[:, :ROWSUMS_ON_SCALAR], in_=sums_scalar[:], func=ACT.Sqrt)
-        nc.scalar.activation(out=root[:, ROWSUMS_ON_SCALAR:], in_=sums_vector[:], func=ACT.Sqrt)
-        d = keep.tile([P, NODE_TILES], F32)
-        nc.vector.reciprocal(out=d[:], in_=root[:])
-        d_repeated = keep.tile([P, NODE_TILES, P], F32)
-        nc.vector.tensor_copy(out=d_repeated[:], in_=d[:].unsqueeze(2).to_broadcast([P, NODE_TILES, P]))
-        d_row = []
-        for h in range(NODES // BANK_F32):
-            d_bank = psum_keep.tile([P, BANK_F32], F32, name="d_row%d" % h)
-            for q in range(BANK_F32 // P):
-                nc.tensor.transpose(
-                    out=d_bank[:, q * P : (q + 1) * P],
-                    in_=d_repeated[:, h * (BANK_F32 // P) + q, :],
-                    identity=ident_f32[:],
-                )
-            d_row.append(d_bank)
+        folded = psum_keep.tile([P, TILES_PER_HALF, P], F32, tag="d_row0")
 
-        for m in range(NODE_TILES):
+        def fold_row_sums(q):
+            for b in range(NODE_TILES):
+                nc.tensor.matmul(
+                    out=folded[:, q, :],
+                    lhsT=ident_bf16[:],
+                    rhs=a_raw[TILES_PER_HALF + q][:, b * P : (b + 1) * P],
+                    start=(b == 0),
+                    stop=(b == NODE_TILES - 1),
+                )
+
+        d = keep.tile([P, NODE_TILES], F32)
+        d_row = []
+
+        def finish_folded_sums():
+            sums_vector = keep.tile([P, TILES_PER_HALF], F32)
+            nc.vector.tensor_reduce(out=sums_vector[:], in_=folded[:], axis=mybir.AxisListType.X, op=ALU.add)
+            nc.scalar.activation(out=root[:, TILES_PER_HALF:], in_=sums_vector[:], func=ACT.Sqrt)
+
+        def degree_factors():
+            nc.vector.reciprocal(out=d[:], in_=root[:])
+            repeated = keep.tile([P, NODE_TILES, P], F32)
+            nc.vector.tensor_copy(out=repeated[:], in_=d[:].unsqueeze(2).to_broadcast([P, NODE_TILES, P]))
+            for g in range(HALVES):
+                d_bank = psum_keep.tile([P, K_PASS], F32, tag="d_row%d" % g)
+                for q in range(TILES_PER_HALF):
+                    nc.tensor.transpose(
+                        out=d_bank[:, q * P : (q + 1) * P],
+                        in_=repeated[:, TILES_PER_HALF * g + q, :],
+                        identity=ident_f32[:],
+                    )
+                d_row.append(d_bank)
+
+        Z_BANKS = HALVES * OUT_CHUNKS
+        for bank in range(Z_BANKS_AHEAD):
+            first_product(bank)
+        for bank in range(Z_BANKS):
+            if bank + Z_BANKS_AHEAD < Z_BANKS:
+                first_product(bank + Z_BANKS_AHEAD)
+            if bank < TILES_PER_HALF:
+                fold_row_sums(bank)
+            add_bias(bank)
+            if bank == OUT_CHUNKS - 1:
+                quantise_z(0)
+            if bank == TILES_PER_HALF + 1:
+                finish_folded_sums()
+            if bank == TILES_PER_HALF + 2:
+                degree_factors()
+        quantise_z(1)
+
+        a_grouped = {}
+        y = {}
+        y_small = {}
+
+        def scale_and_transpose(m):
             a_hat = work.tile([P, NODES], BF16)
-            for h in range(NODES // BANK_F32):
-                j_cols = slice(h * BANK_F32, (h + 1) * BANK_F32)
+            for g in range(HALVES):
+                j_cols = slice(g * K_PASS, (g + 1) * K_PASS)
                 nc.vector.scalar_tensor_tensor(
                     out=a_hat[:, j_cols],
                     in0=a_raw[m][:, j_cols],
                     scalar=d[:, m : m + 1],
-                    in1=d_row[h][:],
+                    in1=d_row[g][:],
                     op0=ALU.mult,
                     op1=ALU.mult,
                 )
-            a_t = psum.tile([P, NODE_PASSES, PACK, P], BF16, tag="transposed")
-            for g in range(NODE_PASSES):
+            a_t = psum.tile([P, HALVES, PACK, P], BF16, tag="transposed")
+            for g in range(HALVES):
                 for t in range(PACK):
-                    j0 = (PACK * g + t) * P
+                    j0 = g * K_PASS + t * P
                     nc.tensor.transpose(out=a_t[:, g, t, :], in_=a_hat[:, j0 : j0 + P], identity=ident_bf16[:])
-            a_grouped = work.tile([P, NODE_PASSES, P, PACK], BF16, align_bytes=64)
-            nc.scalar.copy(out=a_grouped[:], in_=a_t[:].rearrange("p g t i -> p g i t"))
-            a_codes = work.tile([P, NODE_PASSES, P], U32, align_bytes=64)
-            a_scales = work.tile([P, NODE_PASSES, P], U8, align_bytes=64)
+            a_grouped[m] = work.tile([P, HALVES, P, PACK], BF16, align_bytes=64, name="a_grouped")
+            nc.scalar.copy(out=a_grouped[m][:], in_=a_t[:].rearrange("p g t i -> p g i t"))
+
+        def quantise_and_multiply(m):
+            a_codes = work.tile([P, HALVES, P], U32, align_bytes=64)
+            a_scales = work.tile([P, HALVES, P], U8, align_bytes=64)
             nc.vector.quantize_mx(
                 out=a_codes[:].rearrange("p g i -> p (g i)").bitcast(FP8X4),
                 scales=a_scales[:].rearrange("p g i -> p (g i)"),
-                in_=a_grouped[:].rearrange("p g i t -> p (g i t)"),
+                in_=a_grouped[m][:].rearrange("p g i t -> p (g i t)"),
             )
-            y = psum.tile([P, OUTS], F32, tag="product")
-            for g in range(NODE_PASSES):
+            y[m] = psum.tile([P, OUTS], F32, tag="product", name="y")
+            for g in range(HALVES):
                 nc.tensor.matmul_mx(
-                    out=y[:],
+                    out=y[m][:],
                     lhsT=a_codes[:, g, :].bitcast(FP8X4),
                     lhsT_scale=a_scales[:, g, :],
                     rhs=z_codes[:, g, :].bitcast(FP8X4),
                     rhs_scale=z_scales[:, g, :],
                     start=(g == 0),
-                    stop=(g == NODE_PASSES - 1),
+                    stop=(g == HALVES - 1),
                 )
-            y_small = work.tile([P, OUTS], F32)
-            nc.scalar.mul(out=y_small[:], in_=y[:], mul=LEAKY_SLOPE)
+            y_small[m] = work.tile([P, OUTS], F32, name="y_small")
+            nc.scalar.mul(out=y_small[m][:], in_=y[m][:], mul=LEAKY_SLOPE)
+
+        def leaky_relu_and_store(m):
             result = work.tile([P, OUTS], F32)
-            nc.vector.tensor_tensor(out=result[:], in0=y[:], in1=y_small[:], op=ALU.max)
+            nc.vector.tensor_tensor(out=result[:], in0=y[m][:], in1=y_small[m][:], op=ALU.max)
             nc.sync.dma_start(out=out[m * P : (m + 1) * P, :], in_=result[:])
+
+        for step in range(NODE_TILES + QUANTISE_LAG + RELU_LAG):
+            if step < NODE_TILES:
+                scale_and_transpose(step)
+            if 0 <= step - QUANTISE_LAG < NODE_TILES:
+                quantise_and_multiply(step - QUANTISE_LAG)
+            if 0 <= step - QUANTISE_LAG - RELU_LAG:
+                leaky_relu_and_store(step - QUANTISE_LAG - RELU_LAG)

@@ -23,8 +23,8 @@ TILES_PER_HALF = NODE_TILES // HALVES
 OUT_CHUNKS = OUTS // P
 LEAKY_SLOPE = 0.01
 Z_BANKS_AHEAD = 2
-QUANTISE_LAG = 2
-RELU_LAG = 2
+QUANTISE_LAG = 3
+RELU_LAG = 3
 
 FLOPS = 2 * NODES * FEATS * OUTS + 2 * NODES * NODES * OUTS
 
@@ -33,8 +33,9 @@ def tile_gcnlayer_pb_kernel(tc, A1, Hn, Wout, bout, out):
     nc = tc.nc
     with ExitStack() as ctx:
         keep = ctx.enter_context(tc.tile_pool(name="keep", bufs=1))
-        work = ctx.enter_context(tc.tile_pool(name="work", bufs=3))
-        psum = ctx.enter_context(tc.psum_pool(name="psum", bufs=3))
+        work = ctx.enter_context(tc.tile_pool(name="work", bufs=4))
+        psum_transposed = ctx.enter_context(tc.psum_pool(name="psum_transposed", bufs=2))
+        psum_product = ctx.enter_context(tc.psum_pool(name="psum_product", bufs=4))
         psum_keep = ctx.enter_context(tc.psum_pool(name="psum_keep", bufs=1))
         ctx.enter_context(tc.manual_schedule())
 
@@ -57,54 +58,44 @@ def tile_gcnlayer_pb_kernel(tc, A1, Hn, Wout, bout, out):
         w_raw = keep.tile([P, PACK, OUTS], BF16)
         hn_raw = keep.tile([P, NODE_TILES, FEATS], BF16)
         hn_view = Hn.rearrange("(n p) k -> p n k", p=P)
-        nc.sync.dma_start(out=bias_padded[0:1, :], in_=bout.unsqueeze(0))
+
+        def load_hn(pair):
+            nc.sync.dma_start(out=hn_raw[:, 2 * pair : 2 * pair + 2, :], in_=hn_view[:, 2 * pair : 2 * pair + 2, :])
+
+        load_hn(0)
+        load_hn(1)
         nc.sync.dma_start(
             out=w_raw[:].rearrange("q (u e) c -> q u e c", u=2),
             in_=Wout.rearrange("(u q e) c -> q u e c", u=2, e=2),
         )
-        for half in range(HALVES):
-            tiles = slice(TILES_PER_HALF * half, TILES_PER_HALF * (half + 1))
-            nc.sync.dma_start(out=hn_raw[:, tiles, :], in_=hn_view[:, tiles, :])
-        for m in range(NODE_TILES):
-            nc.sync.dma_start(out=a_raw[m][:], in_=A1[m * P : (m + 1) * P, :])
-
-        bias_bank = psum.tile([P, OUTS], F32, tag="product")
-        nc.tensor.matmul(out=bias_bank[:], lhsT=ones_bf16[:], rhs=bias_padded[:], start=True, stop=True)
-        bias = keep.tile([P, OUTS], F32)
-        nc.scalar.copy(out=bias[:], in_=bias_bank[:])
-
-        w_grouped = keep.tile([P, OUTS, PACK], BF16, align_bytes=64)
-        nc.vector.tensor_copy(
-            out=w_grouped[:].rearrange("p (c i) t -> p c t i", i=4),
-            in_=w_raw[:].rearrange("p t (c i) -> p c t i", i=4),
-        )
-        w_codes = keep.tile([P, OUTS], U32, align_bytes=64)
-        w_scales = keep.tile([P, OUTS], U8, align_bytes=64)
-        nc.vector.quantize_mx(
-            out=w_codes[:].bitcast(FP8X4),
-            scales=w_scales[:],
-            in_=w_grouped[:].rearrange("p c t -> p (c t)"),
-        )
+        nc.sync.dma_start(out=bias_padded[0:1, :], in_=bout.unsqueeze(0))
+        load_hn(2)
+        load_hn(3)
+        for q in range(TILES_PER_HALF):
+            for m in (q, TILES_PER_HALF + q):
+                nc.sync.dma_start(out=a_raw[m][:], in_=A1[m * P : (m + 1) * P, :])
 
         hn_words = hn_raw[:].bitcast(F32)
         hn_grouped = keep.tile([P, NODE_TILES, P, PACK], BF16, align_bytes=64)
         hn_grouped_words = hn_grouped[:].bitcast(F32)
         hn_codes = keep.tile([P, NODES], U32, align_bytes=64)
         hn_scales = keep.tile([P, NODES], U8, align_bytes=64)
-        for half in range(HALVES):
-            for pair in range(2 * half, 2 * half + 2):
-                hn_t = psum.tile([P, 2, 2, P], F32, tag="transposed")
-                for n2 in range(2):
-                    for u in range(2):
-                        nc.tensor.transpose(
-                            out=hn_t[:, n2, u, :],
-                            in_=hn_words[:, 2 * pair + n2, u * P : (u + 1) * P],
-                            identity=ident_f32[:],
-                        )
-                nc.scalar.copy(
-                    out=hn_grouped_words[:, 2 * pair : 2 * pair + 2, :, :],
-                    in_=hn_t[:].rearrange("p n u r -> p n r u"),
-                )
+
+        def transpose_hn(pair):
+            hn_t = psum_transposed.tile([P, 2, 2, P], F32, tag="transposed")
+            for n2 in range(2):
+                for u in range(2):
+                    nc.tensor.transpose(
+                        out=hn_t[:, n2, u, :],
+                        in_=hn_words[:, 2 * pair + n2, u * P : (u + 1) * P],
+                        identity=ident_f32[:],
+                    )
+            nc.scalar.copy(
+                out=hn_grouped_words[:, 2 * pair : 2 * pair + 2, :, :],
+                in_=hn_t[:].rearrange("p n u r -> p n r u"),
+            )
+
+        def quantise_hn(half):
             cols = slice(half * K_PASS, (half + 1) * K_PASS)
             nc.vector.quantize_mx(
                 out=hn_codes[:, cols].bitcast(FP8X4),
@@ -114,12 +105,38 @@ def tile_gcnlayer_pb_kernel(tc, A1, Hn, Wout, bout, out):
                 ),
             )
 
-        root = keep.tile([P, NODE_TILES], F32)
-        sums_scalar = keep.tile([P, TILES_PER_HALF], F32)
-        for m in range(TILES_PER_HALF):
-            unread = work.tile([P, NODES], BF16)
-            nc.scalar.activation(out=unread[:], in_=a_raw[m][:], func=ACT.Copy, accum_out=sums_scalar[:, m : m + 1])
-        nc.scalar.activation(out=root[:, :TILES_PER_HALF], in_=sums_scalar[:], func=ACT.Sqrt)
+        w_grouped = keep.tile([P, OUTS, PACK], BF16, align_bytes=64)
+        w_codes = keep.tile([P, OUTS], U32, align_bytes=64)
+        w_scales = keep.tile([P, OUTS], U8, align_bytes=64)
+
+        def regroup_w(half):
+            cols = slice(half * (OUTS // 2), (half + 1) * (OUTS // 2))
+            nc.vector.tensor_copy(
+                out=w_grouped[:, cols, :].rearrange("p (c i) t -> p c t i", i=4),
+                in_=w_raw[:, :, cols].rearrange("p t (c i) -> p c t i", i=4),
+            )
+
+        def quantise_w(half):
+            cols = slice(half * (OUTS // 2), (half + 1) * (OUTS // 2))
+            nc.vector.quantize_mx(
+                out=w_codes[:, cols].bitcast(FP8X4),
+                scales=w_scales[:, cols],
+                in_=w_grouped[:, cols, :].rearrange("p c t -> p (c t)"),
+            )
+
+        transpose_hn(0)
+        transpose_hn(1)
+        regroup_w(0)
+        quantise_hn(0)
+        quantise_w(0)
+
+        bias_bank = psum_product.tile([P, OUTS], F32, tag="product")
+        nc.tensor.matmul(out=bias_bank[:], lhsT=ones_bf16[:], rhs=bias_padded[:], start=True, stop=True)
+        bias = keep.tile([P, OUTS], F32)
+        nc.scalar.copy(out=bias[:], in_=bias_bank[:])
+
+        transpose_hn(2)
+        transpose_hn(3)
 
         z_grouped = keep.tile([P, HALVES, OUTS, PACK], BF16, align_bytes=64)
         z_codes = keep.tile([P, HALVES, OUTS], U32, align_bytes=64)
@@ -128,7 +145,7 @@ def tile_gcnlayer_pb_kernel(tc, A1, Hn, Wout, bout, out):
 
         def first_product(bank):
             g, c = divmod(bank, OUT_CHUNKS)
-            z_bank = psum.tile([P, PACK, P], F32, tag="product")
+            z_bank = psum_product.tile([P, PACK, P], F32, tag="product")
             for t in range(PACK):
                 n_cols = slice((PACK * g + t) * P, (PACK * g + t + 1) * P)
                 nc.tensor.matmul_mx(
@@ -171,13 +188,21 @@ def tile_gcnlayer_pb_kernel(tc, A1, Hn, Wout, bout, out):
                     stop=(b == NODE_TILES - 1),
                 )
 
+        sums = keep.tile([P, NODE_TILES], F32)
+        root = keep.tile([P, NODE_TILES], F32)
         d = keep.tile([P, NODE_TILES], F32)
         d_row = []
 
         def finish_folded_sums():
-            sums_vector = keep.tile([P, TILES_PER_HALF], F32)
-            nc.vector.tensor_reduce(out=sums_vector[:], in_=folded[:], axis=mybir.AxisListType.X, op=ALU.add)
-            nc.scalar.activation(out=root[:, TILES_PER_HALF:], in_=sums_vector[:], func=ACT.Sqrt)
+            unread_folded = keep.tile([P, TILES_PER_HALF, P], BF16)
+            for q in range(TILES_PER_HALF):
+                nc.scalar.activation(
+                    out=unread_folded[:, q, :],
+                    in_=folded[:, q, :],
+                    func=ACT.Copy,
+                    accum_out=sums[:, TILES_PER_HALF + q : TILES_PER_HALF + q + 1],
+                )
+            nc.scalar.activation(out=root[:], in_=sums[:], func=ACT.Sqrt)
 
         def degree_factors():
             nc.vector.reciprocal(out=d[:], in_=root[:])
@@ -196,18 +221,24 @@ def tile_gcnlayer_pb_kernel(tc, A1, Hn, Wout, bout, out):
         Z_BANKS = HALVES * OUT_CHUNKS
         for bank in range(Z_BANKS_AHEAD):
             first_product(bank)
+        regroup_w(1)
+        quantise_w(1)
+        for m in range(TILES_PER_HALF):
+            unread = work.tile([P, NODES], BF16)
+            nc.scalar.activation(out=unread[:], in_=a_raw[m][:], func=ACT.Copy, accum_out=sums[:, m : m + 1])
         for bank in range(Z_BANKS):
             if bank + Z_BANKS_AHEAD < Z_BANKS:
                 first_product(bank + Z_BANKS_AHEAD)
             if bank < TILES_PER_HALF:
                 fold_row_sums(bank)
+            if bank == 1:
+                quantise_hn(1)
             add_bias(bank)
             if bank == OUT_CHUNKS - 1:
                 quantise_z(0)
-            if bank == TILES_PER_HALF + 1:
+            if bank == TILES_PER_HALF:
                 finish_folded_sums()
-            if bank == TILES_PER_HALF + 2:
-                degree_factors()
+        degree_factors()
         quantise_z(1)
 
         a_grouped = {}
@@ -226,7 +257,7 @@ def tile_gcnlayer_pb_kernel(tc, A1, Hn, Wout, bout, out):
                     op0=ALU.mult,
                     op1=ALU.mult,
                 )
-            a_t = psum.tile([P, HALVES, PACK, P], BF16, tag="transposed")
+            a_t = psum_transposed.tile([P, HALVES, PACK, P], BF16, tag="transposed")
             for g in range(HALVES):
                 for t in range(PACK):
                     j0 = g * K_PASS + t * P
@@ -242,7 +273,7 @@ def tile_gcnlayer_pb_kernel(tc, A1, Hn, Wout, bout, out):
                 scales=a_scales[:].rearrange("p g i -> p (g i)"),
                 in_=a_grouped[m][:].rearrange("p g i t -> p (g i t)"),
             )
-            y[m] = psum.tile([P, OUTS], F32, tag="product", name="y")
+            y[m] = psum_product.tile([P, OUTS], F32, tag="product", name="y")
             for g in range(HALVES):
                 nc.tensor.matmul_mx(
                     out=y[m][:],

@@ -39,12 +39,13 @@ def tile_gcnlayer_pb_kernel(tc, A1, Hn, Wout, bout, out):
         psum_keep = ctx.enter_context(tc.psum_pool(name="psum_keep", bufs=1))
         ctx.enter_context(tc.manual_schedule())
 
+        bias_padded = keep.tile([P, OUTS], BF16)
+        nc.vector.memset(bias_padded[:], 0.0)
+        nc.scalar.dma_start(out=bias_padded[0:1, :], in_=bout.unsqueeze(0))
         one = keep.tile([P, 1], F32)
         nc.vector.memset(one[:], 1.0)
         warm = keep.tile([P, 1], F32)
         nc.scalar.activation(out=warm[:], in_=one[:], func=ACT.Sqrt)
-        bias_padded = keep.tile([P, OUTS], BF16)
-        nc.vector.memset(bias_padded[:], 0.0)
         ones_bf16 = keep.tile([P, P], BF16)
         nc.vector.memset(ones_bf16[:], 1.0)
         ident_f32 = keep.tile([P, P], F32)
@@ -68,7 +69,6 @@ def tile_gcnlayer_pb_kernel(tc, A1, Hn, Wout, bout, out):
             out=w_raw[:].rearrange("q (u e) c -> q u e c", u=2),
             in_=Wout.rearrange("(u q e) c -> q u e c", u=2, e=2),
         )
-        nc.sync.dma_start(out=bias_padded[0:1, :], in_=bout.unsqueeze(0))
         load_hn(2)
         load_hn(3)
         for q in range(TILES_PER_HALF):
@@ -238,7 +238,8 @@ def tile_gcnlayer_pb_kernel(tc, A1, Hn, Wout, bout, out):
                 quantise_z(0)
             if bank == TILES_PER_HALF:
                 finish_folded_sums()
-        degree_factors()
+            if bank == Z_BANKS - 2:
+                degree_factors()
         quantise_z(1)
 
         a_grouped = {}

@@ -34,18 +34,19 @@ def tile_gcnlayer_pb_kernel(tc, A1, Hn, Wout, bout, out):
     with ExitStack() as ctx:
         keep = ctx.enter_context(tc.tile_pool(name="keep", bufs=1))
         work = ctx.enter_context(tc.tile_pool(name="work", bufs=4))
+        results = ctx.enter_context(tc.tile_pool(name="results", bufs=NODE_TILES))
         psum_transposed = ctx.enter_context(tc.psum_pool(name="psum_transposed", bufs=2))
         psum_product = ctx.enter_context(tc.psum_pool(name="psum_product", bufs=4))
         psum_keep = ctx.enter_context(tc.psum_pool(name="psum_keep", bufs=1))
         ctx.enter_context(tc.manual_schedule())
 
-        bias_padded = keep.tile([P, OUTS], BF16)
-        nc.vector.memset(bias_padded[:], 0.0)
-        nc.scalar.dma_start(out=bias_padded[0:1, :], in_=bout.unsqueeze(0))
         one = keep.tile([P, 1], F32)
         nc.vector.memset(one[:], 1.0)
         warm = keep.tile([P, 1], F32)
-        nc.scalar.activation(out=warm[:], in_=one[:], func=ACT.Sqrt)
+        nc.scalar.activation(out=warm[:], in_=one[:], func=ACT.Abs_reciprocal_sqrt)
+        bias_padded = keep.tile([P, OUTS], BF16)
+        nc.vector.memset(bias_padded[:], 0.0)
+        nc.scalar.dma_start(out=bias_padded[0:1, :], in_=bout.unsqueeze(0))
         ones_bf16 = keep.tile([P, P], BF16)
         nc.vector.memset(ones_bf16[:], 1.0)
         ident_f32 = keep.tile([P, P], F32)
@@ -58,10 +59,12 @@ def tile_gcnlayer_pb_kernel(tc, A1, Hn, Wout, bout, out):
         a_raw = [keep.tile([P, NODES], BF16, name="a_raw%d" % m) for m in range(NODE_TILES)]
         w_raw = keep.tile([P, PACK, OUTS], BF16)
         hn_raw = keep.tile([P, NODE_TILES, FEATS], BF16)
-        hn_view = Hn.rearrange("(n p) k -> p n k", p=P)
 
         def load_hn(pair):
-            nc.sync.dma_start(out=hn_raw[:, 2 * pair : 2 * pair + 2, :], in_=hn_view[:, 2 * pair : 2 * pair + 2, :])
+            nc.sync.dma_start(
+                out=hn_raw[:, 2 * pair : 2 * pair + 2, :],
+                in_=Hn[2 * P * pair : 2 * P * (pair + 1), :].rearrange("(p e) k -> p e k", e=2),
+            )
 
         load_hn(0)
         load_hn(1)
@@ -188,35 +191,28 @@ def tile_gcnlayer_pb_kernel(tc, A1, Hn, Wout, bout, out):
                     stop=(b == NODE_TILES - 1),
                 )
 
-        sums = keep.tile([P, NODE_TILES], F32)
-        root = keep.tile([P, NODE_TILES], F32)
-        d = keep.tile([P, NODE_TILES], F32)
+        sums = [keep.tile([P, TILES_PER_HALF], F32, name="sums%d" % g) for g in range(HALVES)]
+        d_repeated = keep.tile([P, NODE_TILES, P], F32)
         d_row = []
 
         def finish_folded_sums():
-            unread_folded = keep.tile([P, TILES_PER_HALF, P], BF16)
-            for q in range(TILES_PER_HALF):
-                nc.scalar.activation(
-                    out=unread_folded[:, q, :],
-                    in_=folded[:, q, :],
-                    func=ACT.Copy,
-                    accum_out=sums[:, TILES_PER_HALF + q : TILES_PER_HALF + q + 1],
-                )
-            nc.scalar.activation(out=root[:], in_=sums[:], func=ACT.Sqrt)
+            nc.vector.tensor_reduce(out=sums[1][:], in_=folded[:], axis=mybir.AxisListType.X, op=ALU.add)
 
-        def degree_factors():
-            nc.vector.reciprocal(out=d[:], in_=root[:])
-            repeated = keep.tile([P, NODE_TILES, P], F32)
-            nc.vector.tensor_copy(out=repeated[:], in_=d[:].unsqueeze(2).to_broadcast([P, NODE_TILES, P]))
-            for g in range(HALVES):
-                d_bank = psum_keep.tile([P, K_PASS], F32, tag="d_row%d" % g)
-                for q in range(TILES_PER_HALF):
-                    nc.tensor.transpose(
-                        out=d_bank[:, q * P : (q + 1) * P],
-                        in_=repeated[:, TILES_PER_HALF * g + q, :],
-                        identity=ident_f32[:],
-                    )
-                d_row.append(d_bank)
+        def degree_factors(g):
+            tiles = slice(TILES_PER_HALF * g, TILES_PER_HALF * (g + 1))
+            nc.scalar.activation(
+                out=d_repeated[:, tiles, :],
+                in_=sums[g][:].unsqueeze(2).to_broadcast([P, TILES_PER_HALF, P]),
+                func=ACT.Abs_reciprocal_sqrt,
+            )
+            d_bank = psum_keep.tile([P, K_PASS], F32, tag="d_row%d" % g)
+            for q in range(TILES_PER_HALF):
+                nc.tensor.transpose(
+                    out=d_bank[:, q * P : (q + 1) * P],
+                    in_=d_repeated[:, TILES_PER_HALF * g + q, :],
+                    identity=ident_f32[:],
+                )
+            d_row.append(d_bank)
 
         Z_BANKS = HALVES * OUT_CHUNKS
         for bank in range(Z_BANKS_AHEAD):
@@ -225,7 +221,7 @@ def tile_gcnlayer_pb_kernel(tc, A1, Hn, Wout, bout, out):
         quantise_w(1)
         for m in range(TILES_PER_HALF):
             unread = work.tile([P, NODES], BF16)
-            nc.scalar.activation(out=unread[:], in_=a_raw[m][:], func=ACT.Copy, accum_out=sums[:, m : m + 1])
+            nc.scalar.activation(out=unread[:], in_=a_raw[m][:], func=ACT.Copy, accum_out=sums[0][:, m : m + 1])
         for bank in range(Z_BANKS):
             if bank + Z_BANKS_AHEAD < Z_BANKS:
                 first_product(bank + Z_BANKS_AHEAD)
@@ -238,9 +234,9 @@ def tile_gcnlayer_pb_kernel(tc, A1, Hn, Wout, bout, out):
                 quantise_z(0)
             if bank == TILES_PER_HALF:
                 finish_folded_sums()
-            if bank == Z_BANKS - 2:
-                degree_factors()
         quantise_z(1)
+        for g in range(HALVES):
+            degree_factors(g)
 
         a_grouped = {}
         y = {}
@@ -253,18 +249,19 @@ def tile_gcnlayer_pb_kernel(tc, A1, Hn, Wout, bout, out):
                 nc.vector.scalar_tensor_tensor(
                     out=a_hat[:, j_cols],
                     in0=a_raw[m][:, j_cols],
-                    scalar=d[:, m : m + 1],
+                    scalar=d_repeated[:, m, 0:1],
                     in1=d_row[g][:],
                     op0=ALU.mult,
                     op1=ALU.mult,
                 )
-            a_t = psum_transposed.tile([P, HALVES, PACK, P], BF16, tag="transposed")
+            a_hat_words = a_hat[:].bitcast(F32)
+            a_t = psum_transposed.tile([P, HALVES, 2, P], F32, tag="transposed")
             for g in range(HALVES):
-                for t in range(PACK):
-                    j0 = g * K_PASS + t * P
-                    nc.tensor.transpose(out=a_t[:, g, t, :], in_=a_hat[:, j0 : j0 + P], identity=ident_bf16[:])
+                for u in range(2):
+                    w0 = (2 * g + u) * P
+                    nc.tensor.transpose(out=a_t[:, g, u, :], in_=a_hat_words[:, w0 : w0 + P], identity=ident_f32[:])
             a_grouped[m] = work.tile([P, HALVES, P, PACK], BF16, align_bytes=64, name="a_grouped")
-            nc.scalar.copy(out=a_grouped[m][:], in_=a_t[:].rearrange("p g t i -> p g i t"))
+            nc.scalar.copy(out=a_grouped[m][:].bitcast(F32), in_=a_t[:].rearrange("p g u i -> p g i u"))
 
         def quantise_and_multiply(m):
             a_codes = work.tile([P, HALVES, P], U32, align_bytes=64)
@@ -289,7 +286,7 @@ def tile_gcnlayer_pb_kernel(tc, A1, Hn, Wout, bout, out):
             nc.scalar.mul(out=y_small[m][:], in_=y[m][:], mul=LEAKY_SLOPE)
 
         def leaky_relu_and_store(m):
-            result = work.tile([P, OUTS], F32)
+            result = results.tile([P, OUTS], F32)
             nc.vector.tensor_tensor(out=result[:], in0=y[m][:], in1=y_small[m][:], op=ALU.max)
             nc.sync.dma_start(out=out[m * P : (m + 1) * P, :], in_=result[:])
 

@@ -192,7 +192,7 @@ def tile_gcnlayer_pb_kernel(tc, A1, Hn, Wout, bout, out):
                 )
 
         sums = [keep.tile([P, TILES_PER_HALF], F32, name="sums%d" % g) for g in range(HALVES)]
-        d_repeated = keep.tile([P, NODE_TILES, P], F32)
+        d = keep.tile([P, NODE_TILES], F32)
         d_row = []
 
         def finish_folded_sums():
@@ -200,16 +200,12 @@ def tile_gcnlayer_pb_kernel(tc, A1, Hn, Wout, bout, out):
 
         def degree_factors(g):
             tiles = slice(TILES_PER_HALF * g, TILES_PER_HALF * (g + 1))
-            nc.scalar.activation(
-                out=d_repeated[:, tiles, :],
-                in_=sums[g][:].unsqueeze(2).to_broadcast([P, TILES_PER_HALF, P]),
-                func=ACT.Abs_reciprocal_sqrt,
-            )
+            nc.scalar.activation(out=d[:, tiles], in_=sums[g][:], func=ACT.Abs_reciprocal_sqrt)
             d_bank = psum_keep.tile([P, K_PASS], F32, tag="d_row%d" % g)
             for q in range(TILES_PER_HALF):
                 nc.tensor.transpose(
                     out=d_bank[:, q * P : (q + 1) * P],
-                    in_=d_repeated[:, TILES_PER_HALF * g + q, :],
+                    in_=d[:, TILES_PER_HALF * g + q : TILES_PER_HALF * g + q + 1].to_broadcast([P, P]),
                     identity=ident_f32[:],
                 )
             d_row.append(d_bank)
@@ -232,7 +228,7 @@ def tile_gcnlayer_pb_kernel(tc, A1, Hn, Wout, bout, out):
             add_bias(bank)
             if bank == OUT_CHUNKS - 1:
                 quantise_z(0)
-            if bank == TILES_PER_HALF:
+            if bank == TILES_PER_HALF + 1:
                 finish_folded_sums()
         quantise_z(1)
         for g in range(HALVES):
@@ -249,7 +245,7 @@ def tile_gcnlayer_pb_kernel(tc, A1, Hn, Wout, bout, out):
                 nc.vector.scalar_tensor_tensor(
                     out=a_hat[:, j_cols],
                     in0=a_raw[m][:, j_cols],
-                    scalar=d_repeated[:, m, 0:1],
+                    scalar=d[:, m : m + 1],
                     in1=d_row[g][:],
                     op0=ALU.mult,
                     op1=ALU.mult,

@@ -22,7 +22,7 @@ HALVES = NODES // K_PASS
 TILES_PER_HALF = NODE_TILES // HALVES
 OUT_CHUNKS = OUTS // P
 LEAKY_SLOPE = 0.01
-Z_BANKS_AHEAD = 2
+GPSIMD_TILE = NODE_TILES - 1
 QUANTISE_LAG = 3
 RELU_LAG = 3
 
@@ -40,15 +40,12 @@ def tile_gcnlayer_pb_kernel(tc, A1, Hn, Wout, bout, out):
         psum_keep = ctx.enter_context(tc.psum_pool(name="psum_keep", bufs=1))
         ctx.enter_context(tc.manual_schedule())
 
+        bias_columns = keep.tile([P, PACK], BF16)
+        nc.scalar.dma_start(out=bias_columns[:], in_=bout.rearrange("(p t) -> p t", t=PACK))
         one = keep.tile([P, 1], F32)
         nc.vector.memset(one[:], 1.0)
         warm = keep.tile([P, 1], F32)
         nc.scalar.activation(out=warm[:], in_=one[:], func=ACT.Abs_reciprocal_sqrt)
-        bias_padded = keep.tile([P, OUTS], BF16)
-        nc.vector.memset(bias_padded[:], 0.0)
-        nc.scalar.dma_start(out=bias_padded[0:1, :], in_=bout.unsqueeze(0))
-        ones_bf16 = keep.tile([P, P], BF16)
-        nc.vector.memset(ones_bf16[:], 1.0)
         ident_f32 = keep.tile([P, P], F32)
         nc.vector.memset(ident_f32[:], 0.0)
         make_identity(nc, ident_f32[:], nomemset=True)
@@ -74,9 +71,8 @@ def tile_gcnlayer_pb_kernel(tc, A1, Hn, Wout, bout, out):
         )
         load_hn(2)
         load_hn(3)
-        for q in range(TILES_PER_HALF):
-            for m in (q, TILES_PER_HALF + q):
-                nc.sync.dma_start(out=a_raw[m][:], in_=A1[m * P : (m + 1) * P, :])
+        for m in range(NODE_TILES):
+            nc.sync.dma_start(out=a_raw[m][:], in_=A1[m * P : (m + 1) * P, :])
 
         hn_words = hn_raw[:].bitcast(F32)
         hn_grouped = keep.tile([P, NODE_TILES, P, PACK], BF16, align_bytes=64)
@@ -127,27 +123,88 @@ def tile_gcnlayer_pb_kernel(tc, A1, Hn, Wout, bout, out):
                 in_=w_grouped[:, cols, :].rearrange("p c t -> p (c t)"),
             )
 
-        transpose_hn(0)
-        transpose_hn(1)
-        regroup_w(0)
-        quantise_hn(0)
-        quantise_w(0)
-
-        bias_bank = psum_product.tile([P, OUTS], F32, tag="product")
-        nc.tensor.matmul(out=bias_bank[:], lhsT=ones_bf16[:], rhs=bias_padded[:], start=True, stop=True)
         bias = keep.tile([P, OUTS], F32)
-        nc.scalar.copy(out=bias[:], in_=bias_bank[:])
 
-        transpose_hn(2)
-        transpose_hn(3)
+        def spread_bias():
+            bias_bank = psum_product.tile([P, PACK, P], BF16, tag="product")
+            for t in range(PACK):
+                nc.tensor.transpose(
+                    out=bias_bank[:, t, :],
+                    in_=bias_columns[:, t : t + 1].to_broadcast([P, P]),
+                    identity=ident_bf16[:],
+                )
+            nc.scalar.copy(
+                out=bias[:].rearrange("p (n t) -> p n t", t=PACK), in_=bias_bank[:].rearrange("p t n -> p n t")
+            )
 
-        z_grouped = keep.tile([P, HALVES, OUTS, PACK], BF16, align_bytes=64)
-        z_codes = keep.tile([P, HALVES, OUTS], U32, align_bytes=64)
-        z_scales = keep.tile([P, HALVES, OUTS], U8, align_bytes=64)
-        z_banks = []
+        sums = keep.tile([P, NODE_TILES], F32)
+        d = keep.tile([P, NODE_TILES], F32)
+        d_row = []
 
-        def first_product(bank):
-            g, c = divmod(bank, OUT_CHUNKS)
+        def sum_rows_on_scalar(m):
+            unread = work.tile([P, NODES], BF16, name="unread_scalar")
+            nc.scalar.activation(out=unread[:], in_=a_raw[m][:], func=ACT.Copy, accum_out=sums[:, m : m + 1])
+
+        def sum_rows_on_vector(m):
+            unread = work.tile([P, NODES], BF16, name="unread_vector")
+            nc.vector.tensor_scalar(
+                out=unread[:],
+                in0=a_raw[m][:],
+                scalar1=1.0,
+                scalar2=None,
+                op0=ALU.mult,
+                op1=ALU.add,
+                accum_out=sums[:, m : m + 1],
+            )
+
+        FOLDED = 3
+        folded = psum_keep.tile([P, FOLDED, P], F32, tag="d_row1", name="folded")
+
+        def fold_row_sums(m):
+            for b in range(NODE_TILES):
+                nc.tensor.matmul(
+                    out=folded[:, m // 2, :],
+                    lhsT=ident_bf16[:],
+                    rhs=a_raw[m][:, b * P : (b + 1) * P],
+                    start=(b == 0),
+                    stop=(b == NODE_TILES - 1),
+                )
+
+        def finish_folded_sums():
+            nc.vector.tensor_reduce(
+                out=sums[:, 1 : 2 * FOLDED : 2], in_=folded[:], axis=mybir.AxisListType.X, op=ALU.add
+            )
+
+        def inverse_roots():
+            nc.scalar.activation(out=d[:], in_=sums[:], func=ACT.Abs_reciprocal_sqrt)
+
+        def spread_d(bank, g):
+            for q in range(TILES_PER_HALF):
+                m = TILES_PER_HALF * g + q
+                nc.tensor.transpose(
+                    out=bank[:, q * P : (q + 1) * P],
+                    in_=d[:, m : m + 1].to_broadcast([P, P]),
+                    identity=ident_f32[:],
+                )
+
+        def spread_d_for_vector(g):
+            d_bank = psum_keep.tile([P, K_PASS], F32, tag="d_row%d" % g, name="d_bank")
+            spread_d(d_bank, g)
+            d_row.append(d_bank)
+
+        d_row_sbuf = keep.tile([P, NODES], F32)
+
+        def spread_d_for_gpsimd(g):
+            d_bank = psum_transposed.tile([P, K_PASS], F32, tag="transposed", name="d_bank_gpsimd")
+            spread_d(d_bank, g)
+            nc.scalar.copy(out=d_row_sbuf[:, g * K_PASS : (g + 1) * K_PASS], in_=d_bank[:])
+
+        z_grouped = [keep.tile([P, OUTS, PACK], BF16, align_bytes=64, name="z_grouped%d" % g) for g in range(HALVES)]
+        z_codes = [keep.tile([P, OUTS], U32, align_bytes=64, name="z_codes%d" % g) for g in range(HALVES)]
+        z_scales = [keep.tile([P, OUTS], U8, align_bytes=64, name="z_scales%d" % g) for g in range(HALVES)]
+        z_banks = {}
+
+        def first_product(g, c):
             z_bank = psum_product.tile([P, PACK, P], F32, tag="product")
             for t in range(PACK):
                 n_cols = slice((PACK * g + t) * P, (PACK * g + t + 1) * P)
@@ -160,97 +217,60 @@ def tile_gcnlayer_pb_kernel(tc, A1, Hn, Wout, bout, out):
                     start=True,
                     stop=True,
                 )
-            z_banks.append(z_bank)
+            z_banks[g, c] = z_bank
 
-        def add_bias(bank):
-            g, c = divmod(bank, OUT_CHUNKS)
-            o_cols = slice(c * P, (c + 1) * P)
+        def bias_of(c):
+            return bias[:, c * P : (c + 1) * P].unsqueeze(2).to_broadcast([P, P, PACK])
+
+        def add_bias(g, c):
             nc.vector.tensor_tensor(
-                out=z_grouped[:, g, o_cols, :],
-                in0=z_banks[bank][:].rearrange("p t o -> p o t"),
-                in1=bias[:, o_cols].unsqueeze(2).to_broadcast([P, P, PACK]),
+                out=z_grouped[g][:, c * P : (c + 1) * P, :],
+                in0=z_banks[g, c][:].rearrange("p t o -> p o t"),
+                in1=bias_of(c),
                 op=ALU.add,
             )
 
         def quantise_z(g):
             nc.vector.quantize_mx(
-                out=z_codes[:, g, :].bitcast(FP8X4),
-                scales=z_scales[:, g, :],
-                in_=z_grouped[:, g, :, :].rearrange("p o t -> p (o t)"),
+                out=z_codes[g][:].bitcast(FP8X4),
+                scales=z_scales[g][:],
+                in_=z_grouped[g][:].rearrange("p o t -> p (o t)"),
             )
-
-        folded = psum_keep.tile([P, TILES_PER_HALF, P], F32, tag="d_row0")
-
-        def fold_row_sums(q):
-            for b in range(NODE_TILES):
-                nc.tensor.matmul(
-                    out=folded[:, q, :],
-                    lhsT=ident_bf16[:],
-                    rhs=a_raw[TILES_PER_HALF + q][:, b * P : (b + 1) * P],
-                    start=(b == 0),
-                    stop=(b == NODE_TILES - 1),
-                )
-
-        sums = [keep.tile([P, TILES_PER_HALF], F32, name="sums%d" % g) for g in range(HALVES)]
-        d = keep.tile([P, NODE_TILES], F32)
-        d_row = []
-
-        def finish_folded_sums():
-            nc.vector.tensor_reduce(out=sums[1][:], in_=folded[:], axis=mybir.AxisListType.X, op=ALU.add)
-
-        def degree_factors(g):
-            tiles = slice(TILES_PER_HALF * g, TILES_PER_HALF * (g + 1))
-            nc.scalar.activation(out=d[:, tiles], in_=sums[g][:], func=ACT.Abs_reciprocal_sqrt)
-            d_bank = psum_keep.tile([P, K_PASS], F32, tag="d_row%d" % g)
-            for q in range(TILES_PER_HALF):
-                nc.tensor.transpose(
-                    out=d_bank[:, q * P : (q + 1) * P],
-                    in_=d[:, TILES_PER_HALF * g + q : TILES_PER_HALF * g + q + 1].to_broadcast([P, P]),
-                    identity=ident_f32[:],
-                )
-            d_row.append(d_bank)
-
-        Z_BANKS = HALVES * OUT_CHUNKS
-        for bank in range(Z_BANKS_AHEAD):
-            first_product(bank)
-        regroup_w(1)
-        quantise_w(1)
-        for m in range(TILES_PER_HALF):
-            unread = work.tile([P, NODES], BF16)
-            nc.scalar.activation(out=unread[:], in_=a_raw[m][:], func=ACT.Copy, accum_out=sums[0][:, m : m + 1])
-        for bank in range(Z_BANKS):
-            if bank + Z_BANKS_AHEAD < Z_BANKS:
-                first_product(bank + Z_BANKS_AHEAD)
-            if bank < TILES_PER_HALF:
-                fold_row_sums(bank)
-            if bank == 1:
-                quantise_hn(1)
-            add_bias(bank)
-            if bank == OUT_CHUNKS - 1:
-                quantise_z(0)
-            if bank == TILES_PER_HALF + 1:
-                finish_folded_sums()
-        quantise_z(1)
-        for g in range(HALVES):
-            degree_factors(g)
 
         a_grouped = {}
         y = {}
         y_small = {}
 
-        def scale_and_transpose(m):
-            a_hat = work.tile([P, NODES], BF16)
+        a_hat = {}
+
+        def scale(m, g):
+            if m not in a_hat:
+                a_hat[m] = work.tile([P, NODES], BF16, name="a_hat")
+            j_cols = slice(g * K_PASS, (g + 1) * K_PASS)
+            nc.vector.scalar_tensor_tensor(
+                out=a_hat[m][:, j_cols],
+                in0=a_raw[m][:, j_cols],
+                scalar=d[:, m : m + 1],
+                in1=d_row[g][:],
+                op0=ALU.mult,
+                op1=ALU.mult,
+            )
+
+        a_half_scaled = keep.tile([P, NODES], F32)
+
+        def scale_rows_on_scalar(m):
+            nc.scalar.activation(out=a_half_scaled[:], in_=a_raw[m][:], func=ACT.Copy, scale=d[:, m : m + 1])
+
+        def scale_columns_on_gpsimd(m):
+            a_hat[m] = keep.tile([P, NODES], BF16, name="a_hat_gpsimd")
             for g in range(HALVES):
                 j_cols = slice(g * K_PASS, (g + 1) * K_PASS)
-                nc.vector.scalar_tensor_tensor(
-                    out=a_hat[:, j_cols],
-                    in0=a_raw[m][:, j_cols],
-                    scalar=d[:, m : m + 1],
-                    in1=d_row[g][:],
-                    op0=ALU.mult,
-                    op1=ALU.mult,
+                nc.gpsimd.tensor_tensor(
+                    out=a_hat[m][:, j_cols], in0=a_half_scaled[:, j_cols], in1=d_row_sbuf[:, j_cols], op=ALU.mult
                 )
-            a_hat_words = a_hat[:].bitcast(F32)
+
+        def transpose_a(m):
+            a_hat_words = a_hat[m][:].bitcast(F32)
             a_t = psum_transposed.tile([P, HALVES, 2, P], F32, tag="transposed")
             for g in range(HALVES):
                 for u in range(2):
@@ -259,22 +279,27 @@ def tile_gcnlayer_pb_kernel(tc, A1, Hn, Wout, bout, out):
             a_grouped[m] = work.tile([P, HALVES, P, PACK], BF16, align_bytes=64, name="a_grouped")
             nc.scalar.copy(out=a_grouped[m][:].bitcast(F32), in_=a_t[:].rearrange("p g u i -> p g i u"))
 
-        def quantise_and_multiply(m):
-            a_codes = work.tile([P, HALVES, P], U32, align_bytes=64)
-            a_scales = work.tile([P, HALVES, P], U8, align_bytes=64)
+        a_codes = {}
+        a_scales = {}
+
+        def quantise_a(m):
+            a_codes[m] = work.tile([P, HALVES, P], U32, align_bytes=64, name="a_codes")
+            a_scales[m] = work.tile([P, HALVES, P], U8, align_bytes=64, name="a_scales")
             nc.vector.quantize_mx(
-                out=a_codes[:].rearrange("p g i -> p (g i)").bitcast(FP8X4),
-                scales=a_scales[:].rearrange("p g i -> p (g i)"),
+                out=a_codes[m][:].rearrange("p g i -> p (g i)").bitcast(FP8X4),
+                scales=a_scales[m][:].rearrange("p g i -> p (g i)"),
                 in_=a_grouped[m][:].rearrange("p g i t -> p (g i t)"),
             )
+
+        def multiply(m):
             y[m] = psum_product.tile([P, OUTS], F32, tag="product", name="y")
             for g in range(HALVES):
                 nc.tensor.matmul_mx(
                     out=y[m][:],
-                    lhsT=a_codes[:, g, :].bitcast(FP8X4),
-                    lhsT_scale=a_scales[:, g, :],
-                    rhs=z_codes[:, g, :].bitcast(FP8X4),
-                    rhs_scale=z_scales[:, g, :],
+                    lhsT=a_codes[m][:, g, :].bitcast(FP8X4),
+                    lhsT_scale=a_scales[m][:, g, :],
+                    rhs=z_codes[g][:].bitcast(FP8X4),
+                    rhs_scale=z_scales[g][:],
                     start=(g == 0),
                     stop=(g == HALVES - 1),
                 )
@@ -286,10 +311,55 @@ def tile_gcnlayer_pb_kernel(tc, A1, Hn, Wout, bout, out):
             nc.vector.tensor_tensor(out=result[:], in0=y[m][:], in1=y_small[m][:], op=ALU.max)
             nc.sync.dma_start(out=out[m * P : (m + 1) * P, :], in_=result[:])
 
+        transpose_hn(0)
+        transpose_hn(1)
+        spread_bias()
+        regroup_w(0)
+        quantise_w(0)
+        quantise_hn(0)
+        regroup_w(1)
+        quantise_w(1)
+        transpose_hn(2)
+        transpose_hn(3)
+        for m in (0, 2, 4, 6):
+            sum_rows_on_scalar(m)
+        for c in range(3):
+            first_product(0, c)
+        add_bias(0, 0)
+        quantise_hn(1)
+        fold_row_sums(1)
+        first_product(0, 3)
+        add_bias(0, 1)
+        fold_row_sums(3)
+        add_bias(0, 2)
+        first_product(1, 0)
+        add_bias(0, 3)
+        quantise_z(0)
+        fold_row_sums(5)
+        first_product(1, 1)
+        add_bias(1, 0)
+        finish_folded_sums()
+        sum_rows_on_vector(7)
+        first_product(1, 2)
+        first_product(1, 3)
+        for c in range(1, OUT_CHUNKS):
+            add_bias(1, c)
+        quantise_z(1)
+        inverse_roots()
+        for g in range(HALVES):
+            spread_d_for_vector(g)
+        for g in range(HALVES):
+            spread_d_for_gpsimd(g)
+        scale_rows_on_scalar(GPSIMD_TILE)
+        scale_columns_on_gpsimd(GPSIMD_TILE)
         for step in range(NODE_TILES + QUANTISE_LAG + RELU_LAG):
             if step < NODE_TILES:
-                scale_and_transpose(step)
+                if step != GPSIMD_TILE:
+                    for g in range(HALVES):
+                        scale(step, g)
+                transpose_a(step)
             if 0 <= step - QUANTISE_LAG < NODE_TILES:
-                quantise_and_multiply(step - QUANTISE_LAG)
+                quantise_a(step - QUANTISE_LAG)
+                multiply(step - QUANTISE_LAG)
             if 0 <= step - QUANTISE_LAG - RELU_LAG:
                 leaky_relu_and_store(step - QUANTISE_LAG - RELU_LAG)

@@ -230,6 +230,14 @@ def tile_gcnlayer_pb_kernel(tc, A1, Hn, Wout, bout, out):
                 op=ALU.add,
             )
 
+        z_copy = keep.tile([P, P, PACK], F32)
+
+        def add_bias_on_gpsimd(g, c):
+            nc.scalar.copy(out=z_copy[:], in_=z_banks[g, c][:].rearrange("p t o -> p o t"))
+            nc.gpsimd.tensor_tensor(
+                out=z_grouped[g][:, c * P : (c + 1) * P, :], in0=z_copy[:], in1=bias_of(c), op=ALU.add
+            )
+
         def quantise_z(g):
             nc.vector.quantize_mx(
                 out=z_codes[g][:].bitcast(FP8X4),
@@ -308,15 +316,19 @@ def tile_gcnlayer_pb_kernel(tc, A1, Hn, Wout, bout, out):
 
         def leaky_relu_and_store(m):
             result = results.tile([P, OUTS], F32)
-            nc.vector.tensor_tensor(out=result[:], in0=y[m][:], in1=y_small[m][:], op=ALU.max)
-            nc.sync.dma_start(out=out[m * P : (m + 1) * P, :], in_=result[:])
+            parts = 2 if m == NODE_TILES - 1 else 1
+            width = OUTS // parts
+            for part in range(parts):
+                cols = slice(part * width, (part + 1) * width)
+                nc.vector.tensor_tensor(out=result[:, cols], in0=y[m][:, cols], in1=y_small[m][:, cols], op=ALU.max)
+                nc.sync.dma_start(out=out[m * P : (m + 1) * P, cols], in_=result[:, cols])
 
         transpose_hn(0)
         transpose_hn(1)
         spread_bias()
         regroup_w(0)
-        quantise_w(0)
         quantise_hn(0)
+        quantise_w(0)
         regroup_w(1)
         quantise_w(1)
         transpose_hn(2)
@@ -334,17 +346,16 @@ def tile_gcnlayer_pb_kernel(tc, A1, Hn, Wout, bout, out):
         add_bias(0, 2)
         first_product(1, 0)
         add_bias(0, 3)
-        quantise_z(0)
         fold_row_sums(5)
         first_product(1, 1)
-        add_bias(1, 0)
+        add_bias_on_gpsimd(1, 0)
+        quantise_z(0)
         finish_folded_sums()
         sum_rows_on_vector(7)
         first_product(1, 2)
         first_product(1, 3)
         for c in range(1, OUT_CHUNKS):
             add_bias(1, c)
-        quantise_z(1)
         inverse_roots()
         for g in range(HALVES):
             spread_d_for_vector(g)
@@ -358,6 +369,8 @@ def tile_gcnlayer_pb_kernel(tc, A1, Hn, Wout, bout, out):
                     for g in range(HALVES):
                         scale(step, g)
                 transpose_a(step)
+            if step == 0:
+                quantise_z(1)
             if 0 <= step - QUANTISE_LAG < NODE_TILES:
                 quantise_a(step - QUANTISE_LAG)
                 multiply(step - QUANTISE_LAG)

@@ -299,28 +299,37 @@ def tile_gcnlayer_pb_kernel(tc, A1, Hn, Wout, bout, out):
                 in_=a_grouped[m][:].rearrange("p g i t -> p (g i t)"),
             )
 
+        def parts_of(m):
+            parts = 2 if m == NODE_TILES - 1 else 1
+            width = OUTS // parts
+            return [slice(part * width, (part + 1) * width) for part in range(parts)]
+
         def multiply(m):
-            y[m] = psum_product.tile([P, OUTS], F32, tag="product", name="y")
-            for g in range(HALVES):
-                nc.tensor.matmul_mx(
-                    out=y[m][:],
-                    lhsT=a_codes[m][:, g, :].bitcast(FP8X4),
-                    lhsT_scale=a_scales[m][:, g, :],
-                    rhs=z_codes[g][:].bitcast(FP8X4),
-                    rhs_scale=z_scales[g][:],
-                    start=(g == 0),
-                    stop=(g == HALVES - 1),
-                )
+            y[m] = []
             y_small[m] = work.tile([P, OUTS], F32, name="y_small")
-            nc.scalar.mul(out=y_small[m][:], in_=y[m][:], mul=LEAKY_SLOPE)
+            for part, cols in enumerate(parts_of(m)):
+                width = cols.stop - cols.start
+                if part == 0:
+                    bank = psum_product.tile([P, width], F32, tag="product", name="y")
+                else:
+                    bank = psum_transposed.tile([P, width], F32, tag="transposed", name="y")
+                for g in range(HALVES):
+                    nc.tensor.matmul_mx(
+                        out=bank[:],
+                        lhsT=a_codes[m][:, g, :].bitcast(FP8X4),
+                        lhsT_scale=a_scales[m][:, g, :],
+                        rhs=z_codes[g][:, cols].bitcast(FP8X4),
+                        rhs_scale=z_scales[g][:, cols],
+                        start=(g == 0),
+                        stop=(g == HALVES - 1),
+                    )
+                nc.scalar.mul(out=y_small[m][:, cols], in_=bank[:], mul=LEAKY_SLOPE)
+                y[m].append(bank)
 
         def leaky_relu_and_store(m):
             result = results.tile([P, OUTS], F32)
-            parts = 2 if m == NODE_TILES - 1 else 1
-            width = OUTS // parts
-            for part in range(parts):
-                cols = slice(part * width, (part + 1) * width)
-                nc.vector.tensor_tensor(out=result[:, cols], in0=y[m][:, cols], in1=y_small[m][:, cols], op=ALU.max)
+            for bank, cols in zip(y[m], parts_of(m)):
+                nc.vector.tensor_tensor(out=result[:, cols], in0=bank[:], in1=y_small[m][:, cols], op=ALU.max)
                 nc.sync.dma_start(out=out[m * P : (m + 1) * P, cols], in_=result[:, cols])
 
         transpose_hn(0)

from contextlib import ExitStack

import concourse.mybir as mybir
from concourse.masks import make_identity

F32 = mybir.dt.float32
BF16 = mybir.dt.bfloat16
U32 = mybir.dt.uint32
U8 = mybir.dt.uint8
FP8X4 = mybir.dt.float8_e4m3fn_x4
ACT = mybir.ActivationFunctionType
ALU = mybir.AluOpType

P = 128
PACK = 4
K_PASS = P * PACK
NODES = 1024
FEATS = 512
OUTS = 512
NODE_TILES = NODES // P
HALVES = NODES // K_PASS
TILES_PER_HALF = NODE_TILES // HALVES
OUT_CHUNKS = OUTS // P
LEAKY_SLOPE = 0.01
GPSIMD_TILE = NODE_TILES - 1
QUANTISE_LAG = 3
RELU_LAG = 3

FLOPS = 2 * NODES * FEATS * OUTS + 2 * NODES * NODES * OUTS


def tile_gcnlayer_pb_kernel(tc, A1, Hn, Wout, bout, out):
    nc = tc.nc
    with ExitStack() as ctx:
        keep = ctx.enter_context(tc.tile_pool(name="keep", bufs=1))
        work = ctx.enter_context(tc.tile_pool(name="work", bufs=4))
        results = ctx.enter_context(tc.tile_pool(name="results", bufs=NODE_TILES))
        psum_transposed = ctx.enter_context(tc.psum_pool(name="psum_transposed", bufs=2))
        psum_product = ctx.enter_context(tc.psum_pool(name="psum_product", bufs=4))
        psum_keep = ctx.enter_context(tc.psum_pool(name="psum_keep", bufs=1))
        ctx.enter_context(tc.manual_schedule())

        bias_columns = keep.tile([P, PACK], BF16)
        nc.scalar.dma_start(out=bias_columns[:], in_=bout.rearrange("(p t) -> p t", t=PACK))
        one = keep.tile([P, 1], F32)
        nc.vector.memset(one[:], 1.0)
        warm = keep.tile([P, 1], F32)
        nc.scalar.activation(out=warm[:], in_=one[:], func=ACT.Abs_reciprocal_sqrt)
        ident_f32 = keep.tile([P, P], F32)
        nc.vector.memset(ident_f32[:], 0.0)
        make_identity(nc, ident_f32[:], nomemset=True)
        ident_bf16 = keep.tile([P, P], BF16)
        nc.vector.memset(ident_bf16[:], 0.0)
        make_identity(nc, ident_bf16[:], nomemset=True)

        a_raw = [keep.tile([P, NODES], BF16, name="a_raw%d" % m) for m in range(NODE_TILES)]
        w_raw = keep.tile([P, PACK, OUTS], BF16)
        hn_raw = keep.tile([P, NODE_TILES, FEATS], BF16)

        def load_hn(pair):
            nc.sync.dma_start(
                out=hn_raw[:, 2 * pair : 2 * pair + 2, :],
                in_=Hn[2 * P * pair : 2 * P * (pair + 1), :].rearrange("(p e) k -> p e k", e=2),
            )

        load_hn(0)
        load_hn(1)
        nc.sync.dma_start(
            out=w_raw[:].rearrange("q (u e) c -> q u e c", u=2),
            in_=Wout.rearrange("(u q e) c -> q u e c", u=2, e=2),
        )
        load_hn(2)
        load_hn(3)
        for m in range(NODE_TILES):
            nc.sync.dma_start(out=a_raw[m][:], in_=A1[m * P : (m + 1) * P, :])

        hn_words = hn_raw[:].bitcast(F32)
        hn_grouped = keep.tile([P, NODE_TILES, P, PACK], BF16, align_bytes=64)
        hn_grouped_words = hn_grouped[:].bitcast(F32)
        hn_codes = keep.tile([P, NODES], U32, align_bytes=64)
        hn_scales = keep.tile([P, NODES], U8, align_bytes=64)

        def transpose_hn(pair):
            hn_t = psum_transposed.tile([P, 2, 2, P], F32, tag="transposed")
            for n2 in range(2):
                for u in range(2):
                    nc.tensor.transpose(
                        out=hn_t[:, n2, u, :],
                        in_=hn_words[:, 2 * pair + n2, u * P : (u + 1) * P],
                        identity=ident_f32[:],
                    )
            nc.scalar.copy(
                out=hn_grouped_words[:, 2 * pair : 2 * pair + 2, :, :],
                in_=hn_t[:].rearrange("p n u r -> p n r u"),
            )

        def quantise_hn(half):
            cols = slice(half * K_PASS, (half + 1) * K_PASS)
            nc.vector.quantize_mx(
                out=hn_codes[:, cols].bitcast(FP8X4),
                scales=hn_scales[:, cols],
                in_=hn_grouped[:, TILES_PER_HALF * half : TILES_PER_HALF * (half + 1), :, :].rearrange(
                    "p n r t -> p (n r t)"
                ),
            )

        w_grouped = keep.tile([P, OUTS, PACK], BF16, align_bytes=64)
        w_codes = keep.tile([P, OUTS], U32, align_bytes=64)
        w_scales = keep.tile([P, OUTS], U8, align_bytes=64)

        def regroup_w(half):
            cols = slice(half * (OUTS // 2), (half + 1) * (OUTS // 2))
            nc.vector.tensor_copy(
                out=w_grouped[:, cols, :].rearrange("p (c i) t -> p c t i", i=4),
                in_=w_raw[:, :, cols].rearrange("p t (c i) -> p c t i", i=4),
            )

        def quantise_w(half):
            cols = slice(half * (OUTS // 2), (half + 1) * (OUTS // 2))
            nc.vector.quantize_mx(
                out=w_codes[:, cols].bitcast(FP8X4),
                scales=w_scales[:, cols],
                in_=w_grouped[:, cols, :].rearrange("p c t -> p (c t)"),
            )

        bias = keep.tile([P, OUTS], F32)

        def spread_bias():
            bias_bank = psum_product.tile([P, PACK, P], BF16, tag="product")
            for t in range(PACK):
                nc.tensor.transpose(
                    out=bias_bank[:, t, :],
                    in_=bias_columns[:, t : t + 1].to_broadcast([P, P]),
                    identity=ident_bf16[:],
                )
            nc.scalar.copy(
                out=bias[:].rearrange("p (n t) -> p n t", t=PACK), in_=bias_bank[:].rearrange("p t n -> p n t")
            )

        sums = keep.tile([P, NODE_TILES], F32)
        d = keep.tile([P, NODE_TILES], F32)
        d_row = []

        def sum_rows_on_scalar(m):
            unread = work.tile([P, NODES], BF16, name="unread_scalar")
            nc.scalar.activation(out=unread[:], in_=a_raw[m][:], func=ACT.Copy, accum_out=sums[:, m : m + 1])

        def sum_rows_on_vector(m):
            unread = work.tile([P, NODES], BF16, name="unread_vector")
            nc.vector.tensor_scalar(
                out=unread[:],
                in0=a_raw[m][:],
                scalar1=1.0,
                scalar2=None,
                op0=ALU.mult,
                op1=ALU.add,
                accum_out=sums[:, m : m + 1],
            )

        FOLDED = 3
        folded = psum_keep.tile([P, FOLDED, P], F32, tag="d_row1", name="folded")

        def fold_row_sums(m):
            for b in range(NODE_TILES):
                nc.tensor.matmul(
                    out=folded[:, m // 2, :],
                    lhsT=ident_bf16[:],
                    rhs=a_raw[m][:, b * P : (b + 1) * P],
                    start=(b == 0),
                    stop=(b == NODE_TILES - 1),
                )

        def finish_folded_sums():
            nc.vector.tensor_reduce(
                out=sums[:, 1 : 2 * FOLDED : 2], in_=folded[:], axis=mybir.AxisListType.X, op=ALU.add
            )

        def inverse_roots():
            nc.scalar.activation(out=d[:], in_=sums[:], func=ACT.Abs_reciprocal_sqrt)

        def spread_d(bank, g):
            for q in range(TILES_PER_HALF):
                m = TILES_PER_HALF * g + q
                nc.tensor.transpose(
                    out=bank[:, q * P : (q + 1) * P],
                    in_=d[:, m : m + 1].to_broadcast([P, P]),
                    identity=ident_f32[:],
                )

        def spread_d_for_vector(g):
            d_bank = psum_keep.tile([P, K_PASS], F32, tag="d_row%d" % g, name="d_bank")
            spread_d(d_bank, g)
            d_row.append(d_bank)

        d_row_sbuf = keep.tile([P, NODES], F32)

        def spread_d_for_gpsimd(g):
            d_bank = psum_transposed.tile([P, K_PASS], F32, tag="transposed", name="d_bank_gpsimd")
            spread_d(d_bank, g)
            nc.scalar.copy(out=d_row_sbuf[:, g * K_PASS : (g + 1) * K_PASS], in_=d_bank[:])

        z_grouped = [keep.tile([P, OUTS, PACK], BF16, align_bytes=64, name="z_grouped%d" % g) for g in range(HALVES)]
        z_codes = [keep.tile([P, OUTS], U32, align_bytes=64, name="z_codes%d" % g) for g in range(HALVES)]
        z_scales = [keep.tile([P, OUTS], U8, align_bytes=64, name="z_scales%d" % g) for g in range(HALVES)]
        z_banks = {}

        def first_product(g, c):
            z_bank = psum_product.tile([P, PACK, P], F32, tag="product")
            for t in range(PACK):
                n_cols = slice((PACK * g + t) * P, (PACK * g + t + 1) * P)
                nc.tensor.matmul_mx(
                    out=z_bank[:, t, :],
                    lhsT=hn_codes[:, n_cols].bitcast(FP8X4),
                    lhsT_scale=hn_scales[:, n_cols],
                    rhs=w_codes[:, c * P : (c + 1) * P].bitcast(FP8X4),
                    rhs_scale=w_scales[:, c * P : (c + 1) * P],
                    start=True,
                    stop=True,
                )
            z_banks[g, c] = z_bank

        def bias_of(c):
            return bias[:, c * P : (c + 1) * P].unsqueeze(2).to_broadcast([P, P, PACK])

        def add_bias(g, c):
            nc.vector.tensor_tensor(
                out=z_grouped[g][:, c * P : (c + 1) * P, :],
                in0=z_banks[g, c][:].rearrange("p t o -> p o t"),
                in1=bias_of(c),
                op=ALU.add,
            )

        z_copy = keep.tile([P, P, PACK], F32)

        def add_bias_on_gpsimd(g, c):
            nc.scalar.copy(out=z_copy[:], in_=z_banks[g, c][:].rearrange("p t o -> p o t"))
            nc.gpsimd.tensor_tensor(
                out=z_grouped[g][:, c * P : (c + 1) * P, :], in0=z_copy[:], in1=bias_of(c), op=ALU.add
            )

        def quantise_z(g):
            nc.vector.quantize_mx(
                out=z_codes[g][:].bitcast(FP8X4),
                scales=z_scales[g][:],
                in_=z_grouped[g][:].rearrange("p o t -> p (o t)"),
            )

        a_grouped = {}
        y = {}
        y_small = {}

        a_hat = {}

        def scale(m, g):
            if m not in a_hat:
                a_hat[m] = work.tile([P, NODES], BF16, name="a_hat")
            j_cols = slice(g * K_PASS, (g + 1) * K_PASS)
            nc.vector.scalar_tensor_tensor(
                out=a_hat[m][:, j_cols],
                in0=a_raw[m][:, j_cols],
                scalar=d[:, m : m + 1],
                in1=d_row[g][:],
                op0=ALU.mult,
                op1=ALU.mult,
            )

        a_half_scaled = keep.tile([P, NODES], F32)

        def scale_rows_on_scalar(m):
            nc.scalar.activation(out=a_half_scaled[:], in_=a_raw[m][:], func=ACT.Copy, scale=d[:, m : m + 1])

        def scale_columns_on_gpsimd(m):
            a_hat[m] = keep.tile([P, NODES], BF16, name="a_hat_gpsimd")
            for g in range(HALVES):
                j_cols = slice(g * K_PASS, (g + 1) * K_PASS)
                nc.gpsimd.tensor_tensor(
                    out=a_hat[m][:, j_cols], in0=a_half_scaled[:, j_cols], in1=d_row_sbuf[:, j_cols], op=ALU.mult
                )

        def transpose_a(m):
            a_hat_words = a_hat[m][:].bitcast(F32)
            a_t = psum_transposed.tile([P, HALVES, 2, P], F32, tag="transposed")
            for g in range(HALVES):
                for u in range(2):
                    w0 = (2 * g + u) * P
                    nc.tensor.transpose(out=a_t[:, g, u, :], in_=a_hat_words[:, w0 : w0 + P], identity=ident_f32[:])
            a_grouped[m] = work.tile([P, HALVES, P, PACK], BF16, align_bytes=64, name="a_grouped")
            nc.scalar.copy(out=a_grouped[m][:].bitcast(F32), in_=a_t[:].rearrange("p g u i -> p g i u"))

        a_codes = {}
        a_scales = {}

        def quantise_a(m):
            a_codes[m] = work.tile([P, HALVES, P], U32, align_bytes=64, name="a_codes")
            a_scales[m] = work.tile([P, HALVES, P], U8, align_bytes=64, name="a_scales")
            nc.vector.quantize_mx(
                out=a_codes[m][:].rearrange("p g i -> p (g i)").bitcast(FP8X4),
                scales=a_scales[m][:].rearrange("p g i -> p (g i)"),
                in_=a_grouped[m][:].rearrange("p g i t -> p (g i t)"),
            )

        def parts_of(m):
            parts = 2 if m == NODE_TILES - 1 else 1
            width = OUTS // parts
            return [slice(part * width, (part + 1) * width) for part in range(parts)]

        def multiply(m):
            y[m] = []
            y_small[m] = work.tile([P, OUTS], F32, name="y_small")
            for part, cols in enumerate(parts_of(m)):
                width = cols.stop - cols.start
                if part == 0:
                    bank = psum_product.tile([P, width], F32, tag="product", name="y")
                else:
                    bank = psum_transposed.tile([P, width], F32, tag="transposed", name="y")
                for g in range(HALVES):
                    nc.tensor.matmul_mx(
                        out=bank[:],
                        lhsT=a_codes[m][:, g, :].bitcast(FP8X4),
                        lhsT_scale=a_scales[m][:, g, :],
                        rhs=z_codes[g][:, cols].bitcast(FP8X4),
                        rhs_scale=z_scales[g][:, cols],
                        start=(g == 0),
                        stop=(g == HALVES - 1),
                    )
                nc.scalar.mul(out=y_small[m][:, cols], in_=bank[:], mul=LEAKY_SLOPE)
                y[m].append(bank)

        def leaky_relu_and_store(m):
            result = results.tile([P, OUTS], F32)
            for bank, cols in zip(y[m], parts_of(m)):
                nc.vector.tensor_tensor(out=result[:, cols], in0=bank[:], in1=y_small[m][:, cols], op=ALU.max)
                nc.sync.dma_start(out=out[m * P : (m + 1) * P, cols], in_=result[:, cols])

        transpose_hn(0)
        transpose_hn(1)
        spread_bias()
        regroup_w(0)
        quantise_hn(0)
        quantise_w(0)
        regroup_w(1)
        quantise_w(1)
        transpose_hn(2)
        transpose_hn(3)
        for m in (0, 2, 4, 6):
            sum_rows_on_scalar(m)
        for c in range(3):
            first_product(0, c)
        add_bias(0, 0)
        quantise_hn(1)
        fold_row_sums(1)
        first_product(0, 3)
        add_bias(0, 1)
        fold_row_sums(3)
        add_bias(0, 2)
        first_product(1, 0)
        add_bias(0, 3)
        fold_row_sums(5)
        first_product(1, 1)
        add_bias_on_gpsimd(1, 0)
        quantise_z(0)
        finish_folded_sums()
        sum_rows_on_vector(7)
        first_product(1, 2)
        first_product(1, 3)
        for c in range(1, OUT_CHUNKS):
            add_bias(1, c)
        inverse_roots()
        for g in range(HALVES):
            spread_d_for_vector(g)
        for g in range(HALVES):
            spread_d_for_gpsimd(g)
        scale_rows_on_scalar(GPSIMD_TILE)
        scale_columns_on_gpsimd(GPSIMD_TILE)
        for step in range(NODE_TILES + QUANTISE_LAG + RELU_LAG):
            if step < NODE_TILES:
                if step != GPSIMD_TILE:
                    for g in range(HALVES):
                        scale(step, g)
                transpose_a(step)
            if step == 0:
                quantise_z(1)
            if 0 <= step - QUANTISE_LAG < NODE_TILES:
                quantise_a(step - QUANTISE_LAG)
                multiply(step - QUANTISE_LAG)
            if 0 <= step - QUANTISE_LAG - RELU_LAG:
                leaky_relu_and_store(step - QUANTISE_LAG - RELU_LAG)
